import numpy as np
import ml_dtypes


def mxq(x, axis, fmt="e4m3"):
    dtype, down = {"e4m3": (ml_dtypes.float8_e4m3fn, 7), "e5m2": (ml_dtypes.float8_e5m2, 14)}[fmt]
    v = np.moveaxis(np.asarray(x, np.float32).astype(ml_dtypes.bfloat16).astype(np.float64), axis, -1)
    blocks = v.reshape(v.shape[:-1] + (-1, 32))
    amax = np.abs(blocks).max(-1, keepdims=True)
    byte = np.maximum(np.where(amax > 0, np.frexp(amax)[1] - 1 + 127, 0) - down, 1)
    scale = np.exp2(byte - 127.0)
    codes = (blocks / scale).astype(np.float32).astype(dtype).astype(np.float64)
    return np.moveaxis((codes * scale).reshape(v.shape), -1, axis)


WIDE = False


def mx_kscale(k):
    if not WIDE:
        return np.ones(k)
    levels = np.array([10, -10, 5, -5, 0])
    a = np.random.permutation(np.resize(levels, k // 512 * 4)).reshape(k // 512, 4)
    idx = np.arange(k)
    return np.exp2(a[idx // 512, idx % 128 // 32])


BF16 = ml_dtypes.bfloat16


def bf(x):
    return np.asarray(x, np.float32).astype(BF16)


def f64(x):
    return np.asarray(x).astype(np.float64)


E2M1 = np.array([0.0, 0.5, 1.0, 1.5, 2.0, 3.0, 4.0, 6.0, -0.0, -0.5, -1.0, -1.5, -2.0, -3.0, -4.0, -6.0])


def pack_weight(w, fmt):
    k, n = w.shape
    w = f64(bf(w)).reshape(k // 32, 32, n)
    amax = np.abs(w).max(1)
    if fmt == "e4m3":
        byte = np.frexp(amax)[1] - 1 + 127 - 7
    else:
        mant, ex = np.frexp(amax / 6.0)
        byte = np.where(mant > 0.5, ex, ex - 1) + 127
    byte = np.clip(np.where(amax > 0, byte, 1), 1, 254)
    scaled = (w * np.exp2(127.0 - byte)[:, None, :]).reshape(k, n).astype(np.float32)
    by_word = np.ascontiguousarray(scaled.reshape(k // 512, 128, 4, n).transpose(0, 1, 3, 2))
    if fmt == "e4m3":
        words = by_word.astype(ml_dtypes.float8_e4m3fn).view(np.uint8)
    else:
        c = by_word.astype(ml_dtypes.float4_e2m1fn).view(np.uint8) & 0xF
        words = c[..., 0::2] | (c[..., 1::2] << 4)
    return np.ascontiguousarray(words), np.ascontiguousarray(byte.astype(np.uint8).reshape(k // 512, 16, n))


def unpack_weight(words, scales, fmt):
    g, p, n, _ = words.shape
    if fmt == "e4m3":
        vals = np.ascontiguousarray(words).view(ml_dtypes.float8_e4m3fn).astype(np.float64)
    else:
        nib = np.empty((g, p, n, 4), np.uint8)
        nib[..., 0::2] = words & 0xF
        nib[..., 1::2] = words >> 4
        vals = E2M1[nib]
    vals = vals * np.repeat(np.exp2(scales.astype(np.float64) - 127.0), 8, axis=1)[..., None]
    return vals.transpose(0, 1, 3, 2).reshape(g * 512, n)


M, N, H = 128, 3072, 2048
RMIN, RMAX = 0.4, 0.99
FMT = "e4m3"


def half_glorot(rows, cols):
    limit = np.sqrt(1.5 / ((rows + cols) / 2.0))
    return np.random.uniform(-limit, limit, (rows, cols))


def setup_inputs():
    s, t = mx_kscale(N), mx_kscale(H)
    inputs = np.random.standard_normal((M, N))
    state_re = np.random.standard_normal((M, H))
    state_im = np.random.standard_normal((M, H))
    C_re = half_glorot(H, N)
    C_im = half_glorot(H, N)
    B_re = half_glorot(N, H)
    B_im = half_glorot(N, H)
    D = np.random.standard_normal(N)
    nu = np.random.uniform(np.log(-np.log(RMAX)), np.log(-np.log(RMIN)), H)
    theta = np.random.uniform(0.0, 3.14 / 10, H)
    gamma = np.sqrt(1.0 - np.exp(-2.0 * np.exp(nu)))
    B_re_words, B_re_scales = pack_weight(B_re / s[:, None], FMT)
    B_im_words, B_im_scales = pack_weight(B_im / s[:, None], FMT)
    C_re_words, C_re_scales = pack_weight(C_re / t[:, None], FMT)
    C_im_words, C_im_scales = pack_weight(C_im / t[:, None], FMT)
    return {"inputs": bf(inputs * s), "state_re": bf(state_re * t), "state_im": bf(state_im * t),
            "B_re_words": B_re_words, "B_re_scales": B_re_scales,
            "B_im_words": B_im_words, "B_im_scales": B_im_scales,
            "C_re_words": C_re_words, "C_re_scales": C_re_scales,
            "C_im_words": C_im_words, "C_im_scales": C_im_scales,
            "D": bf(D / s), "nu": bf(nu), "theta": bf(theta), "gamma": bf(gamma * t)}


def reference(inputs, state_re, state_im, B_re_words, B_re_scales, B_im_words, B_im_scales,
              C_re_words, C_re_scales, C_im_words, C_im_scales, D, nu, theta, gamma):
    u = f64(inputs)
    mag = np.exp(-np.exp(f64(nu)))
    lam_re = mag * np.cos(f64(theta))
    lam_im = mag * np.sin(f64(theta))
    uq = mxq(u, 1, "e4m3")
    new_u_re = f64(gamma) * (uq @ unpack_weight(B_re_words, B_re_scales, FMT))
    new_u_im = f64(gamma) * (uq @ unpack_weight(B_im_words, B_im_scales, FMT))
    x_re = f64(state_re) * lam_re - f64(state_im) * lam_im + new_u_re
    x_im = f64(state_re) * lam_im + f64(state_im) * lam_re + new_u_im
    y = (mxq(x_re, 1, "e4m3") @ unpack_weight(C_re_words, C_re_scales, FMT)) - (mxq(x_im, 1, "e4m3") @ unpack_weight(C_im_words, C_im_scales, FMT)) + f64(D) * u
    return y, x_re, x_im

@@ -1,0 +1,416 @@
+from contextlib import ExitStack
+
+import concourse.mybir as mybir
+from concourse.masks import make_identity
+
+F32 = mybir.dt.float32
+BF16 = mybir.dt.bfloat16
+U32 = mybir.dt.uint32
+U8 = mybir.dt.uint8
+I32 = mybir.dt.int32
+FP8X4 = mybir.dt.float8_e4m3fn_x4
+ALU = mybir.AluOpType
+ACT = mybir.ActivationFunctionType
+
+P = 128
+N_IN = 3072
+H = 2048
+BANK = 512
+G1 = N_IN // 512
+G2 = H // 512
+NB1 = H // BANK
+NB2 = N_IN // BANK
+B_BUFS = 6
+C_BUFS = 5
+PIECE = 1024
+
+FLOPS = 2 * P * 4 * N_IN * H
+
+
+def tile_linearrecurrentunitcell_w_kernel(
+    tc,
+    inputs,
+    state_re,
+    state_im,
+    B_re_words,
+    B_re_scales,
+    B_im_words,
+    B_im_scales,
+    C_re_words,
+    C_re_scales,
+    C_im_words,
+    C_im_scales,
+    D,
+    nu,
+    theta,
+    gamma,
+    out_0,
+    out_1,
+    out_2,
+):
+    nc = tc.nc
+    b_words = (B_re_words, B_im_words)
+    c_words = (C_re_words, C_im_words)
+    states = (state_re, state_im)
+    x_out = (out_1, out_2)
+
+    with ExitStack() as ctx:
+        const = ctx.enter_context(tc.tile_pool(name="const", bufs=1))
+        work = ctx.enter_context(tc.tile_pool(name="work", bufs=3))
+        wb = ctx.enter_context(tc.tile_pool(name="wb", bufs=B_BUFS))
+        wc = ctx.enter_context(tc.tile_pool(name="wc", bufs=C_BUFS))
+        cp = ctx.enter_context(tc.tile_pool(name="cp", bufs=3))
+        ps = ctx.enter_context(tc.psum_pool(name="ps", bufs=1))
+        ctx.enter_context(tc.manual_schedule())
+
+        scratch_count = [0]
+
+        def scratch(shape, dtype, name):
+            bank = 4 + scratch_count[0] % 4
+            scratch_count[0] += 1
+            return ps.tile(shape, dtype, name=name, tag="b%d" % bank)
+
+        ident_f = const.tile([P, P], F32, name="ident_f")
+        make_identity(nc, ident_f[:])
+        ident_b = const.tile([P, P], BF16, name="ident_b")
+        make_identity(nc, ident_b[:])
+
+        nu_t = const.tile([P, BANK], BF16, name="nu_t")
+        th_t = const.tile([P, BANK], BF16, name="th_t")
+        gd_t = const.tile([P, BANK], BF16, name="gd_t")
+        pb = const.tile([P, 3, H], U8, name="pb", align_bytes=64)
+        pc = const.tile([P, 2, N_IN], U8, name="pc", align_bytes=64)
+        for small in (nu_t, th_t, gd_t):
+            nc.vector.memset(small[:].bitcast(I32), 0)
+        nc.vector.memset(pb[:].rearrange("p s n -> p (s n)").bitcast(I32), 0)
+        nc.vector.memset(pc[:].rearrange("p s n -> p (s n)").bitcast(I32), 0)
+
+        u_sb = const.tile([P, N_IN], BF16, name="u_sb", align_bytes=64)
+        u_grp = const.tile([P, N_IN], BF16, name="u_grp", align_bytes=64)
+        uq_w = const.tile([P, G1 * P], U32, name="uq_w", align_bytes=64)
+        uq_s = const.tile([P, G1 * P], U8, name="uq_s", align_bytes=64)
+        s_sb = [const.tile([P, H], BF16, name="s_sb%d" % part) for part in range(2)]
+        x_sb = [const.tile([P, H], F32, name="x_sb%d" % part) for part in range(2)]
+        xq_w = [const.tile([P, G2 * P], U32, name="xq_w%d" % part, align_bytes=64) for part in range(2)]
+        xq_s = [const.tile([P, G2 * P], U8, name="xq_s%d" % part, align_bytes=64) for part in range(2)]
+        mag = const.tile([P, BANK], F32, name="mag")
+        lam_re = const.tile([P, BANK], F32, name="lam_re")
+        lam_im = const.tile([P, BANK], F32, name="lam_im")
+        gam_b = const.tile([P, H], BF16, name="gam_b")
+        du = const.tile([P, N_IN], F32, name="du")
+
+        nc.sync.dma_start(out=u_sb[:], in_=inputs)
+        nc.scalar.dma_start(out=nu_t[0:4, :], in_=nu.rearrange("(r c) -> r c", c=BANK))
+        nc.scalar.dma_start(out=th_t[0:4, :], in_=theta.rearrange("(r c) -> r c", c=BANK))
+        nc.scalar.dma_start(out=gd_t[0:4, :], in_=gamma.rearrange("(r c) -> r c", c=BANK))
+        nc.scalar.dma_start(out=gd_t[4:10, :], in_=D.rearrange("(r c) -> r c", c=BANK))
+
+        def load_planes(planes, slot, first, count, src, g0):
+            for q in (0, 2, 1, 3):
+                nc.sync.dma_start(
+                    out=planes[32 * q + first : 32 * q + first + 4 * count, slot, :].bitcast(I32),
+                    in_=src[g0 : g0 + count, 4 * q : 4 * q + 4, :].bitcast(I32),
+                )
+
+        load_planes(pb, 0, 0, 4, B_re_scales, 0)
+        load_planes(pb, 2, 0, 2, B_re_scales, 4)
+        load_planes(pb, 2, 8, 2, B_im_scales, 4)
+        load_planes(pb, 1, 0, 4, B_im_scales, 0)
+        load_planes(pc, 0, 0, 4, C_re_scales, 0)
+        load_planes(pc, 1, 0, 4, C_im_scales, 0)
+
+        b_tiles = {}
+        c_tiles = {}
+
+        def load_b(i):
+            part, g = divmod(i, G1)
+            bw = wb.tile([P, H], U32, name="bw", tag="bw", align_bytes=64)
+            nc.sync.dma_start(
+                out=bw[:].bitcast(I32),
+                in_=b_words[part][g].rearrange("p n t -> p (n t)").bitcast(I32),
+            )
+            b_tiles[i] = bw
+
+        def load_c(j):
+            part, g = divmod(j, G2)
+            cw = wc.tile([P, N_IN], U32, name="cw", tag="cw", align_bytes=64)
+            nc.sync.dma_start(
+                out=cw[:].bitcast(I32),
+                in_=c_words[part][g].rearrange("p n t -> p (n t)").bitcast(I32),
+            )
+            c_tiles[j] = cw
+
+        load_b(0)
+        for part in range(2):
+            nc.sync.dma_start(out=s_sb[part][:], in_=states[part])
+        for i in range(1, B_BUFS):
+            load_b(i)
+
+        u_words = u_sb[:].bitcast(F32)
+        u_grp_words = u_grp[:].bitcast(F32)
+
+        def u_transposes(j):
+            ut = scratch([P, 2, 2, P], F32, "ut")
+            for gg in range(2):
+                g = 2 * j + gg
+                for half in range(2):
+                    nc.tensor.transpose(
+                        ut[:, gg, half, :],
+                        u_words[:, 256 * g + half : 256 * (g + 1) : 2],
+                        ident_f[:],
+                    )
+            nc.vector.tensor_copy(
+                out=u_grp_words[:, 512 * j : 512 * (j + 1)].rearrange(
+                    "p (g m h) -> p g m h", g=2, h=2
+                ),
+                in_=ut[:].rearrange("p g h m -> p g m h"),
+            )
+
+        def u_quantise(j):
+            nc.vector.quantize_mx(
+                out=uq_w[:, 256 * j : 256 * (j + 1)].bitcast(FP8X4),
+                scales=uq_s[:, 256 * j : 256 * (j + 1)],
+                in_=u_grp[:, 1024 * j : 1024 * (j + 1)],
+            )
+
+        u_transposes(0)
+        u_transposes(1)
+        u_quantise(0)
+        u_transposes(2)
+        u_quantise(1)
+        u_quantise(2)
+
+        nc.scalar.activation(out=mag[:], in_=nu_t[:], func=ACT.Exp)
+        nc.scalar.activation(out=mag[:], in_=mag[:], func=ACT.Exp, scale=-1.0)
+        nc.scalar.activation(out=lam_im[:], in_=th_t[:], func=ACT.Sin)
+        nc.scalar.activation(out=lam_re[:], in_=th_t[:], func=ACT.Sin, scale=0.5)
+        nc.scalar.activation(out=lam_re[:], in_=lam_re[:], func=ACT.Square)
+        nc.vector.tensor_tensor(out=lam_im[:], in0=lam_im[:], in1=mag[:], op=ALU.mult)
+        nc.vector.tensor_scalar(
+            out=lam_re[:], in0=lam_re[:], scalar1=-2.0, scalar2=1.0, op0=ALU.mult, op1=ALU.add
+        )
+        nc.vector.tensor_tensor(out=lam_re[:], in0=lam_re[:], in1=mag[:], op=ALU.mult)
+
+        lam_banks = {}
+
+        def spread_lambda(c):
+            row = ident_f[:, c : c + 1].to_broadcast([P, P])
+            l_re = scratch([P, BANK], F32, "l_re")
+            nc.tensor.matmul(out=l_re[:], lhsT=row, rhs=lam_re[:], start=True, stop=True)
+            l_im = scratch([P, BANK], F32, "l_im")
+            nc.tensor.matmul(out=l_im[:], lhsT=row, rhs=lam_im[:], start=True, stop=True)
+            lam_banks[c] = (l_re, l_im)
+
+        def rotate_state(c):
+            cols = slice(BANK * c, BANK * (c + 1))
+            l_re, l_im = lam_banks[c]
+            t_re = work.tile([P, BANK], F32, name="t_re", tag="t_rot", bufs=3)
+            t_im = work.tile([P, BANK], F32, name="t_im", tag="t_rot", bufs=3)
+            nc.vector.tensor_tensor(out=x_sb[0][:, cols], in0=l_re[:], in1=s_sb[0][:, cols], op=ALU.mult)
+            nc.vector.tensor_tensor(out=t_im[:], in0=l_re[:], in1=s_sb[1][:, cols], op=ALU.mult)
+            nc.vector.tensor_tensor(out=t_re[:], in0=l_im[:], in1=s_sb[1][:, cols], op=ALU.mult)
+            nc.vector.tensor_tensor(out=x_sb[1][:, cols], in0=l_im[:], in1=s_sb[0][:, cols], op=ALU.mult)
+            nc.vector.tensor_tensor(out=x_sb[0][:, cols], in0=x_sb[0][:, cols], in1=t_re[:], op=ALU.subtract)
+            nc.vector.tensor_tensor(out=x_sb[1][:, cols], in0=x_sb[1][:, cols], in1=t_im[:], op=ALU.add)
+
+        def spread_gamma(c):
+            g_ps = scratch([P, BANK], F32, "g_ps")
+            nc.tensor.matmul(
+                out=g_ps[:],
+                lhsT=ident_b[:, c : c + 1].to_broadcast([P, P]),
+                rhs=gd_t[:],
+                start=True,
+                stop=True,
+            )
+            nc.scalar.copy(out=gam_b[:, BANK * c : BANK * (c + 1)], in_=g_ps[:])
+
+        acc = {}
+
+        def b_plane(part, g):
+            if g < 4:
+                return part, 4 * g
+            return 2, 8 * part + 4 * (g - 4)
+
+        def stage1(i):
+            part, g = divmod(i, G1)
+            if g == 0:
+                for n in range(NB1):
+                    acc[(part, n)] = ps.tile([P, BANK], F32, name="acc", tag="b%d" % n)
+            slot, k = b_plane(part, g)
+            for n in range(NB1):
+                cols = slice(BANK * n, BANK * (n + 1))
+                nc.tensor.matmul_mx(
+                    out=acc[(part, n)][:],
+                    lhsT=uq_w[:, P * g : P * (g + 1)].bitcast(FP8X4),
+                    lhsT_scale=uq_s[:, P * g : P * (g + 1)],
+                    rhs=b_tiles[i][:, cols].bitcast(FP8X4),
+                    rhs_scale=pb[k:P, slot, cols],
+                    start=(g == 0),
+                    stop=(g == G1 - 1),
+                )
+            if i + B_BUFS < 2 * G1:
+                load_b(i + B_BUFS)
+
+        scaled = {}
+
+        def scale_by_gamma(part, n):
+            cols = slice(BANK * n, BANK * (n + 1))
+            sc = work.tile([P, BANK], F32, name="sc", tag="sc", bufs=4)
+            nc.vector.tensor_tensor(out=sc[:], in0=acc[(part, n)][:], in1=gam_b[:, cols], op=ALU.mult)
+            scaled[(part, n)] = sc
+
+        x_t = {}
+
+        def finish_x(part, n):
+            cols = slice(BANK * n, BANK * (n + 1))
+            nc.vector.tensor_tensor(
+                out=x_sb[part][:, cols], in0=scaled[(part, n)][:], in1=x_sb[part][:, cols], op=ALU.add
+            )
+            x_bf = work.tile([P, BANK], BF16, name="x_bf", tag="x_bf", bufs=3)
+            nc.scalar.activation(
+                out=x_bf[:], in_=x_sb[part][:, cols], func=ACT.Copy, scale=(1.0 if part == 0 else -1.0)
+            )
+            if part == 0:
+                xt = scratch([P, 4, P], BF16, "xt")
+            else:
+                xt = ps.tile([P, 4, P], BF16, name="xt", tag="b%d" % (6 + n % 2))
+            for t in range(4):
+                nc.tensor.transpose(xt[:, t, :], x_bf[:, t:BANK:4], ident_b[:])
+            x_t[(part, n)] = xt
+
+        def quantise_x(part, n):
+            x_grp = work.tile([P, BANK], BF16, name="x_grp", tag="x_grp", bufs=3, align_bytes=64)
+            nc.scalar.copy(
+                out=x_grp[:].rearrange("p (m t) -> p m t", t=4),
+                in_=x_t[(part, n)][:].rearrange("p t m -> p m t"),
+            )
+            nc.vector.quantize_mx(
+                out=xq_w[part][:, P * n : P * (n + 1)].bitcast(FP8X4),
+                scales=xq_s[part][:, P * n : P * (n + 1)],
+                in_=x_grp[:],
+            )
+
+        y_acc = {}
+
+        def open_y():
+            for n in range(NB2):
+                y_acc[n] = ps.tile([P, BANK], F32, name="y_acc", tag="b%d" % n)
+
+        def stage2_pass(j, n, words):
+            part, g = divmod(j, G2)
+            nc.tensor.matmul_mx(
+                out=y_acc[n][:],
+                lhsT=xq_w[part][:, P * g : P * (g + 1)].bitcast(FP8X4),
+                lhsT_scale=xq_s[part][:, P * g : P * (g + 1)],
+                rhs=words.bitcast(FP8X4),
+                rhs_scale=pc[4 * g : P, part, BANK * n : BANK * (n + 1)],
+                start=(j == 0),
+                stop=(j == 2 * G2 - 1),
+            )
+
+        def stage2(j):
+            for n in range(NB2):
+                stage2_pass(j, n, c_tiles[j][:, BANK * n : BANK * (n + 1)])
+
+        def skip_term(c):
+            cols = slice(BANK * c, BANK * (c + 1))
+            d_ps = ps.tile([P, BANK], F32, name="d_ps", tag="b%d" % (6 + c % 2))
+            nc.tensor.matmul(
+                out=d_ps[:],
+                lhsT=ident_b[:, 4 + c : 5 + c].to_broadcast([P, P]),
+                rhs=gd_t[:],
+                start=True,
+                stop=True,
+            )
+            nc.vector.tensor_tensor(out=du[:, cols], in0=d_ps[:], in1=u_sb[:, cols], op=ALU.mult)
+
+        def finish_y(n):
+            cols = slice(BANK * n, BANK * (n + 1))
+            y_sb = work.tile([P, BANK], F32, name="y_sb", tag="y_sb", bufs=4)
+            nc.vector.tensor_tensor(out=y_sb[:], in0=y_acc[n][:], in1=du[:, cols], op=ALU.add)
+            nc.sync.dma_start(out=out_0[:, cols], in_=y_sb[:])
+
+        spread_lambda(0)
+        spread_lambda(1)
+        rotate_state(0)
+        stage1(0)
+        spread_lambda(2)
+        rotate_state(1)
+        stage1(1)
+        spread_lambda(3)
+        rotate_state(2)
+        stage1(2)
+        rotate_state(3)
+        spread_gamma(0)
+        spread_gamma(1)
+        stage1(3)
+        spread_gamma(2)
+        spread_gamma(3)
+        stage1(4)
+        stage1(5)
+        for j in range(C_BUFS):
+            load_c(j)
+
+        for n in range(NB1):
+            scale_by_gamma(0, n)
+        stage1(6)
+        finish_x(0, 0)
+        stage1(7)
+        finish_x(0, 1)
+        quantise_x(0, 0)
+        stage1(8)
+        finish_x(0, 2)
+        quantise_x(0, 1)
+        stage1(9)
+        finish_x(0, 3)
+        quantise_x(0, 2)
+        quantise_x(0, 3)
+        stage1(10)
+        stage1(11)
+
+        for n in range(NB1):
+            scale_by_gamma(1, n)
+        open_y()
+        finish_x(1, 0)
+        finish_x(1, 1)
+        quantise_x(1, 0)
+        stage2(0)
+        load_c(5)
+        finish_x(1, 2)
+        quantise_x(1, 1)
+        finish_x(1, 3)
+        quantise_x(1, 2)
+        quantise_x(1, 3)
+        stage2(1)
+        load_c(6)
+        last = 2 * G2 - 1
+        pieces = []
+        for k in range(N_IN // PIECE):
+            piece = cp.tile([P, PIECE], U32, name="piece", tag="piece", align_bytes=64)
+            nc.sync.dma_start(
+                out=piece[:].bitcast(I32),
+                in_=c_words[1][G2 - 1]
+                .rearrange("p n t -> p (n t)")[:, 4 * PIECE * k : 4 * PIECE * (k + 1)]
+                .bitcast(I32),
+            )
+            pieces.append(piece)
+        for part in range(2):
+            nc.sync.dma_start(out=x_out[part], in_=x_sb[part][:])
+        skip_term(0)
+        skip_term(1)
+        stage2(2)
+        skip_term(2)
+        skip_term(3)
+        stage2(3)
+        skip_term(4)
+        skip_term(5)
+        stage2(4)
+        stage2(5)
+        stage2(6)
+        per_piece = PIECE // BANK
+        for k in range(N_IN // PIECE):
+            for r in range(per_piece):
+                n = per_piece * k + r
+                stage2_pass(last, n, pieces[k][:, BANK * r : BANK * (r + 1)])
+            for r in range(per_piece):
+                finish_y(per_piece * k + r)

@@ -73,10 +73,9 @@ def tile_linearrecurrentunitcell_w_kernel(
         ident_f = const.tile([P, P], F32, name="ident_f")
         make_identity(nc, ident_f[:])
         ident_b = const.tile([P, P], BF16, name="ident_b")
-        make_identity(nc, ident_b[:])
 
-        nu_t = const.tile([P, BANK], BF16, name="nu_t")
-        th_t = const.tile([P, BANK], BF16, name="th_t")
+        nu_t = const.tile([P, P], BF16, name="nu_t")
+        th_t = const.tile([P, P], BF16, name="th_t")
         gd_t = const.tile([P, BANK], BF16, name="gd_t")
         pb = const.tile([P, 3, H], U8, name="pb", align_bytes=64)
         pc = const.tile([P, 2, N_IN], U8, name="pc", align_bytes=64)
@@ -93,29 +92,31 @@ def tile_linearrecurrentunitcell_w_kernel(
         x_sb = [const.tile([P, H], F32, name="x_sb%d" % part) for part in range(2)]
         xq_w = [const.tile([P, G2 * P], U32, name="xq_w%d" % part, align_bytes=64) for part in range(2)]
         xq_s = [const.tile([P, G2 * P], U8, name="xq_s%d" % part, align_bytes=64) for part in range(2)]
-        mag = const.tile([P, BANK], F32, name="mag")
-        lam_re = const.tile([P, BANK], F32, name="lam_re")
-        lam_im = const.tile([P, BANK], F32, name="lam_im")
+        mag = const.tile([P, P], F32, name="mag")
+        lam_re = const.tile([P, P], F32, name="lam_re")
+        lam_im = const.tile([P, P], F32, name="lam_im")
+        lam_col = const.tile([P, 2, H // P], F32, name="lam_col")
         gam_b = const.tile([P, H], BF16, name="gam_b")
         du = const.tile([P, N_IN], F32, name="du")
 
         nc.sync.dma_start(out=u_sb[:], in_=inputs)
-        nc.scalar.dma_start(out=nu_t[0:4, :], in_=nu.rearrange("(r c) -> r c", c=BANK))
-        nc.scalar.dma_start(out=th_t[0:4, :], in_=theta.rearrange("(r c) -> r c", c=BANK))
+        nc.scalar.dma_start(out=nu_t[0 : H // P, :], in_=nu.rearrange("(r c) -> r c", c=P))
+        nc.scalar.dma_start(out=th_t[0 : H // P, :], in_=theta.rearrange("(r c) -> r c", c=P))
         nc.scalar.dma_start(out=gd_t[0:4, :], in_=gamma.rearrange("(r c) -> r c", c=BANK))
         nc.scalar.dma_start(out=gd_t[4:10, :], in_=D.rearrange("(r c) -> r c", c=BANK))
 
         def load_planes(planes, slot, first, count, src, g0):
             for q in (0, 2, 1, 3):
-                nc.sync.dma_start(
-                    out=planes[32 * q + first : 32 * q + first + 4 * count, slot, :].bitcast(I32),
-                    in_=src[g0 : g0 + count, 4 * q : 4 * q + 4, :].bitcast(I32),
+                nc.gpsimd.dma_start(
+                    out=planes[32 * q + first : 32 * q + first + 4 * count, slot, :].bitcast(F32),
+                    in_=src[g0 : g0 + count, 4 * q : 4 * q + 4, :].bitcast(F32),
                 )
 
         load_planes(pb, 0, 0, 4, B_re_scales, 0)
+        make_identity(nc, ident_b[:])
         load_planes(pb, 2, 0, 2, B_re_scales, 4)
-        load_planes(pb, 2, 8, 2, B_im_scales, 4)
         load_planes(pb, 1, 0, 4, B_im_scales, 0)
+        load_planes(pb, 2, 8, 2, B_im_scales, 4)
         load_planes(pc, 0, 0, 4, C_re_scales, 0)
         load_planes(pc, 1, 0, 4, C_im_scales, 0)
 
@@ -191,15 +192,25 @@ def tile_linearrecurrentunitcell_w_kernel(
         )
         nc.vector.tensor_tensor(out=lam_re[:], in0=lam_re[:], in1=mag[:], op=ALU.mult)
 
+        lam_ps = scratch([P, 2, P], F32, "lam_ps")
+        nc.tensor.transpose(lam_ps[:, 0, :], lam_re[:], ident_f[:])
+        nc.tensor.transpose(lam_ps[:, 1, :], lam_im[:], ident_f[:])
+        nc.vector.tensor_copy(out=lam_col[:], in_=lam_ps[:, :, 0 : H // P])
+
         lam_banks = {}
 
         def spread_lambda(c):
-            row = ident_f[:, c : c + 1].to_broadcast([P, P])
-            l_re = scratch([P, BANK], F32, "l_re")
-            nc.tensor.matmul(out=l_re[:], lhsT=row, rhs=lam_re[:], start=True, stop=True)
-            l_im = scratch([P, BANK], F32, "l_im")
-            nc.tensor.matmul(out=l_im[:], lhsT=row, rhs=lam_im[:], start=True, stop=True)
-            lam_banks[c] = (l_re, l_im)
+            banks = []
+            for part in range(2):
+                bank = scratch([P, BANK], F32, "lam_bank")
+                for r in range(4):
+                    nc.tensor.transpose(
+                        bank[:, P * r : P * (r + 1)],
+                        lam_col[:, part, 4 * c + r : 4 * c + r + 1].to_broadcast([P, P]),
+                        ident_f[:],
+                    )
+                banks.append(bank)
+            lam_banks[c] = banks
 
         def rotate_state(c):
             cols = slice(BANK * c, BANK * (c + 1))
@@ -330,83 +341,60 @@ def tile_linearrecurrentunitcell_w_kernel(
             nc.vector.tensor_tensor(out=y_sb[:], in0=y_acc[n][:], in1=du[:, cols], op=ALU.add)
             nc.sync.dma_start(out=out_0[:, cols], in_=y_sb[:])
 
-        spread_lambda(0)
-        spread_lambda(1)
-        rotate_state(0)
-        stage1(0)
-        spread_lambda(2)
-        rotate_state(1)
-        stage1(1)
-        spread_lambda(3)
-        rotate_state(2)
-        stage1(2)
-        rotate_state(3)
-        spread_gamma(0)
-        spread_gamma(1)
-        stage1(3)
-        spread_gamma(2)
-        spread_gamma(3)
-        stage1(4)
-        stage1(5)
+        for g in range(G1):
+            if g < NB1:
+                spread_lambda(g)
+            stage1(g)
+            if g < NB1:
+                rotate_state(g)
+            else:
+                spread_gamma(2 * (g - NB1))
+                spread_gamma(2 * (g - NB1) + 1)
         for j in range(C_BUFS):
             load_c(j)
 
         for n in range(NB1):
             scale_by_gamma(0, n)
-        stage1(6)
-        finish_x(0, 0)
-        stage1(7)
-        finish_x(0, 1)
-        quantise_x(0, 0)
-        stage1(8)
-        finish_x(0, 2)
-        quantise_x(0, 1)
-        stage1(9)
-        finish_x(0, 3)
-        quantise_x(0, 2)
-        quantise_x(0, 3)
-        stage1(10)
-        stage1(11)
+        for g in range(G1):
+            stage1(G1 + g)
+            if g < NB1:
+                finish_x(0, g)
+            if 1 <= g <= NB1:
+                quantise_x(0, g - 1)
 
         for n in range(NB1):
             scale_by_gamma(1, n)
         open_y()
-        finish_x(1, 0)
-        finish_x(1, 1)
-        quantise_x(1, 0)
-        stage2(0)
-        load_c(5)
-        finish_x(1, 2)
-        quantise_x(1, 1)
-        finish_x(1, 3)
-        quantise_x(1, 2)
-        quantise_x(1, 3)
-        stage2(1)
-        load_c(6)
         last = 2 * G2 - 1
         pieces = []
-        for k in range(N_IN // PIECE):
-            piece = cp.tile([P, PIECE], U32, name="piece", tag="piece", align_bytes=64)
-            nc.sync.dma_start(
-                out=piece[:].bitcast(I32),
-                in_=c_words[1][G2 - 1]
-                .rearrange("p n t -> p (n t)")[:, 4 * PIECE * k : 4 * PIECE * (k + 1)]
-                .bitcast(I32),
-            )
-            pieces.append(piece)
-        for part in range(2):
-            nc.sync.dma_start(out=x_out[part], in_=x_sb[part][:])
-        skip_term(0)
-        skip_term(1)
-        stage2(2)
-        skip_term(2)
-        skip_term(3)
-        stage2(3)
-        skip_term(4)
-        skip_term(5)
-        stage2(4)
-        stage2(5)
-        stage2(6)
+
+        def load_pieces():
+            for k in range(N_IN // PIECE):
+                piece = cp.tile([P, PIECE], U32, name="piece", tag="piece", align_bytes=64)
+                nc.sync.dma_start(
+                    out=piece[:].bitcast(I32),
+                    in_=c_words[1][G2 - 1]
+                    .rearrange("p n t -> p (n t)")[:, 4 * PIECE * k : 4 * PIECE * (k + 1)]
+                    .bitcast(I32),
+                )
+                pieces.append(piece)
+
+        for j in range(last):
+            stage2(j)
+            if j + C_BUFS < last:
+                load_c(j + C_BUFS)
+            if j + C_BUFS == last:
+                load_pieces()
+            if j < NB1:
+                finish_x(1, j)
+            if j == NB1 - 1:
+                for part in range(2):
+                    nc.sync.dma_start(out=x_out[part], in_=x_sb[part][:])
+            if 1 <= j <= NB1:
+                quantise_x(1, j - 1)
+            if j >= NB1:
+                skip_term(2 * (j - NB1))
+                skip_term(2 * (j - NB1) + 1)
         per_piece = PIECE // BANK
         for k in range(N_IN // PIECE):
             for r in range(per_piece):

@@ -107,9 +107,9 @@ def tile_linearrecurrentunitcell_w_kernel(
 
         def load_planes(planes, slot, first, count, src, g0):
             for q in (0, 2, 1, 3):
-                nc.gpsimd.dma_start(
-                    out=planes[32 * q + first : 32 * q + first + 4 * count, slot, :].bitcast(F32),
-                    in_=src[g0 : g0 + count, 4 * q : 4 * q + 4, :].bitcast(F32),
+                nc.sync.dma_start(
+                    out=planes[32 * q + first : 32 * q + first + 4 * count, slot, :].bitcast(I32),
+                    in_=src[g0 : g0 + count, 4 * q : 4 * q + 4, :].bitcast(I32),
                 )
 
         load_planes(pb, 0, 0, 4, B_re_scales, 0)

@@ -385,16 +385,16 @@ def tile_linearrecurrentunitcell_w_kernel(
                 load_c(j + C_BUFS)
             if j + C_BUFS == last:
                 load_pieces()
-            if j < NB1:
-                finish_x(1, j)
-            if j == NB1 - 1:
                 for part in range(2):
                     nc.sync.dma_start(out=x_out[part], in_=x_sb[part][:])
-            if 1 <= j <= NB1:
-                quantise_x(1, j - 1)
-            if j >= NB1:
-                skip_term(2 * (j - NB1))
-                skip_term(2 * (j - NB1) + 1)
+            if j < 2:
+                finish_x(1, 2 * j)
+                finish_x(1, 2 * j + 1)
+                quantise_x(1, 2 * j)
+                quantise_x(1, 2 * j + 1)
+            elif j < 5:
+                skip_term(2 * (j - 2))
+                skip_term(2 * (j - 2) + 1)
         per_piece = PIECE // BANK
         for k in range(N_IN // PIECE):
             for r in range(per_piece):

@@ -125,7 +125,7 @@ def tile_linearrecurrentunitcell_w_kernel(
 
         def load_b(i):
             part, g = divmod(i, G1)
-            bw = wb.tile([P, H], U32, name="bw", tag="bw", align_bytes=64)
+            bw = wb.tile([P, H], U32, name="bw", tag="bw", align_bytes=256)
             nc.sync.dma_start(
                 out=bw[:].bitcast(I32),
                 in_=b_words[part][g].rearrange("p n t -> p (n t)").bitcast(I32),
@@ -134,7 +134,7 @@ def tile_linearrecurrentunitcell_w_kernel(
 
         def load_c(j):
             part, g = divmod(j, G2)
-            cw = wc.tile([P, N_IN], U32, name="cw", tag="cw", align_bytes=64)
+            cw = wc.tile([P, N_IN], U32, name="cw", tag="cw", align_bytes=256)
             nc.sync.dma_start(
                 out=cw[:].bitcast(I32),
                 in_=c_words[part][g].rearrange("p n t -> p (n t)").bitcast(I32),
@@ -337,7 +337,7 @@ def tile_linearrecurrentunitcell_w_kernel(
 
         def finish_y(n):
             cols = slice(BANK * n, BANK * (n + 1))
-            y_sb = work.tile([P, BANK], F32, name="y_sb", tag="y_sb", bufs=4)
+            y_sb = work.tile([P, BANK], F32, name="y_sb", tag="y_sb", bufs=4, align_bytes=256)
             nc.vector.tensor_tensor(out=y_sb[:], in0=y_acc[n][:], in1=du[:, cols], op=ALU.add)
             nc.sync.dma_start(out=out_0[:, cols], in_=y_sb[:])
 
@@ -370,7 +370,7 @@ def tile_linearrecurrentunitcell_w_kernel(
 
         def load_pieces():
             for k in range(N_IN // PIECE):
-                piece = cp.tile([P, PIECE], U32, name="piece", tag="piece", align_bytes=64)
+                piece = cp.tile([P, PIECE], U32, name="piece", tag="piece", align_bytes=256)
                 nc.sync.dma_start(
                     out=piece[:].bitcast(I32),
                     in_=c_words[1][G2 - 1]

@@ -117,8 +117,17 @@ def tile_linearrecurrentunitcell_w_kernel(
         load_planes(pb, 2, 0, 2, B_re_scales, 4)
         load_planes(pb, 1, 0, 4, B_im_scales, 0)
         load_planes(pb, 2, 8, 2, B_im_scales, 4)
-        load_planes(pc, 0, 0, 4, C_re_scales, 0)
-        load_planes(pc, 1, 0, 4, C_im_scales, 0)
+
+        def load_planes_by_row(planes, slot, src):
+            for r in range(4):
+                for q in (0, 2, 1, 3):
+                    nc.gpsimd.dma_start(
+                        out=planes[32 * q + r : 32 * q + 16 : 4, slot, :].bitcast(F32),
+                        in_=src[:, 4 * q + r, :].bitcast(F32),
+                    )
+
+        load_planes_by_row(pc, 0, C_re_scales)
+        load_planes_by_row(pc, 1, C_im_scales)
 
         b_tiles = {}
         c_tiles = {}

@@ -117,17 +117,8 @@ def tile_linearrecurrentunitcell_w_kernel(
         load_planes(pb, 2, 0, 2, B_re_scales, 4)
         load_planes(pb, 1, 0, 4, B_im_scales, 0)
         load_planes(pb, 2, 8, 2, B_im_scales, 4)
-
-        def load_planes_by_row(planes, slot, src):
-            for r in range(4):
-                for q in (0, 2, 1, 3):
-                    nc.gpsimd.dma_start(
-                        out=planes[32 * q + r : 32 * q + 16 : 4, slot, :].bitcast(F32),
-                        in_=src[:, 4 * q + r, :].bitcast(F32),
-                    )
-
-        load_planes_by_row(pc, 0, C_re_scales)
-        load_planes_by_row(pc, 1, C_im_scales)
+        load_planes(pc, 0, 0, 4, C_re_scales, 0)
+        load_planes(pc, 1, 0, 4, C_im_scales, 0)
 
         b_tiles = {}
         c_tiles = {}
@@ -344,11 +335,17 @@ def tile_linearrecurrentunitcell_w_kernel(
             )
             nc.vector.tensor_tensor(out=du[:, cols], in0=d_ps[:], in1=u_sb[:, cols], op=ALU.mult)
 
-        def finish_y(n):
-            cols = slice(BANK * n, BANK * (n + 1))
-            y_sb = work.tile([P, BANK], F32, name="y_sb", tag="y_sb", bufs=4, align_bytes=256)
-            nc.vector.tensor_tensor(out=y_sb[:], in0=y_acc[n][:], in1=du[:, cols], op=ALU.add)
-            nc.sync.dma_start(out=out_0[:, cols], in_=y_sb[:])
+        def finish_y(k):
+            y_sb = work.tile([P, PIECE], F32, name="y_sb", tag="y_sb", bufs=3, align_bytes=256)
+            for r in range(PIECE // BANK):
+                n = (PIECE // BANK) * k + r
+                nc.vector.tensor_tensor(
+                    out=y_sb[:, BANK * r : BANK * (r + 1)],
+                    in0=y_acc[n][:],
+                    in1=du[:, BANK * n : BANK * (n + 1)],
+                    op=ALU.add,
+                )
+            nc.sync.dma_start(out=out_0[:, PIECE * k : PIECE * (k + 1)], in_=y_sb[:])
 
         for g in range(G1):
             if g < NB1:
@@ -409,5 +406,4 @@ def tile_linearrecurrentunitcell_w_kernel(
             for r in range(per_piece):
                 n = per_piece * k + r
                 stage2_pass(last, n, pieces[k][:, BANK * r : BANK * (r + 1)])
-            for r in range(per_piece):
-                finish_y(per_piece * k + r)
+            finish_y(k)

@@ -77,19 +77,19 @@ def tile_linearrecurrentunitcell_w_kernel(
         nu_t = const.tile([P, P], BF16, name="nu_t")
         th_t = const.tile([P, P], BF16, name="th_t")
         gd_t = const.tile([P, BANK], BF16, name="gd_t")
-        pb = const.tile([P, 3, H], U8, name="pb", align_bytes=64)
-        pc = const.tile([P, 2, N_IN], U8, name="pc", align_bytes=64)
+        pb = const.tile([P, 3, H], U8, name="pb", align_bytes=256)
+        pc = const.tile([P, 2, N_IN], U8, name="pc", align_bytes=256)
         for small in (nu_t, th_t, gd_t):
             nc.vector.memset(small[:].bitcast(I32), 0)
         nc.vector.memset(pb[:].rearrange("p s n -> p (s n)").bitcast(I32), 0)
         nc.vector.memset(pc[:].rearrange("p s n -> p (s n)").bitcast(I32), 0)
 
-        u_sb = const.tile([P, N_IN], BF16, name="u_sb", align_bytes=64)
+        u_sb = const.tile([P, N_IN], BF16, name="u_sb", align_bytes=256)
         u_grp = const.tile([P, N_IN], BF16, name="u_grp", align_bytes=64)
         uq_w = const.tile([P, G1 * P], U32, name="uq_w", align_bytes=64)
         uq_s = const.tile([P, G1 * P], U8, name="uq_s", align_bytes=64)
-        s_sb = [const.tile([P, H], BF16, name="s_sb%d" % part) for part in range(2)]
-        x_sb = [const.tile([P, H], F32, name="x_sb%d" % part) for part in range(2)]
+        s_sb = [const.tile([P, H], BF16, name="s_sb%d" % part, align_bytes=256) for part in range(2)]
+        x_sb = [const.tile([P, H], F32, name="x_sb%d" % part, align_bytes=256) for part in range(2)]
         xq_w = [const.tile([P, G2 * P], U32, name="xq_w%d" % part, align_bytes=64) for part in range(2)]
         xq_s = [const.tile([P, G2 * P], U8, name="xq_s%d" % part, align_bytes=64) for part in range(2)]
         mag = const.tile([P, P], F32, name="mag")

@@ -20,9 +20,10 @@ G1 = N_IN // 512
 G2 = H // 512
 NB1 = H // BANK
 NB2 = N_IN // BANK
-B_BUFS = 6
-C_BUFS = 5
 PIECE = 1024
+B_BYTES = 4 * H
+C_BYTES = 4 * N_IN
+RING = 15 * B_BYTES
 
 FLOPS = 2 * P * 4 * N_IN * H
 
@@ -57,9 +58,7 @@ def tile_linearrecurrentunitcell_w_kernel(
     with ExitStack() as ctx:
         const = ctx.enter_context(tc.tile_pool(name="const", bufs=1))
         work = ctx.enter_context(tc.tile_pool(name="work", bufs=3))
-        wb = ctx.enter_context(tc.tile_pool(name="wb", bufs=B_BUFS))
-        wc = ctx.enter_context(tc.tile_pool(name="wc", bufs=C_BUFS))
-        cp = ctx.enter_context(tc.tile_pool(name="cp", bufs=3))
+        ring = ctx.enter_context(tc.tile_pool(name="ring", bufs=1))
         ps = ctx.enter_context(tc.psum_pool(name="ps", bufs=1))
         ctx.enter_context(tc.manual_schedule())
 
@@ -125,26 +124,31 @@ def tile_linearrecurrentunitcell_w_kernel(
 
         def load_b(i):
             part, g = divmod(i, G1)
-            bw = wb.tile([P, H], U32, name="bw", tag="bw", align_bytes=256)
+            bw = ring.tile([P, 2, H], U32, name="bw%d" % i, tag="bw%d" % i, align_bytes=256, offset=B_BYTES * i)
             nc.sync.dma_start(
                 out=bw[:].bitcast(I32),
-                in_=b_words[part][g].rearrange("p n t -> p (n t)").bitcast(I32),
+                in_=b_words[part][g : g + 2].rearrange("g p n t -> p g (n t)").bitcast(I32),
             )
-            b_tiles[i] = bw
+            for r in range(2):
+                b_tiles[i + r] = bw[:, r, :]
 
-        def load_c(j):
+        def load_c(j, count):
             part, g = divmod(j, G2)
-            cw = wc.tile([P, N_IN], U32, name="cw", tag="cw", align_bytes=256)
+            cw = ring.tile(
+                [P, count, N_IN], U32, name="cw%d" % j, tag="cw%d" % j, align_bytes=256,
+                offset=(2 * G1 * B_BYTES + j * C_BYTES) % RING,
+            )
             nc.sync.dma_start(
                 out=cw[:].bitcast(I32),
-                in_=c_words[part][g].rearrange("p n t -> p (n t)").bitcast(I32),
+                in_=c_words[part][g : g + count].rearrange("g p n t -> p g (n t)").bitcast(I32),
             )
-            c_tiles[j] = cw
+            for r in range(count):
+                c_tiles[j + r] = cw[:, r, :]
 
         load_b(0)
         for part in range(2):
             nc.sync.dma_start(out=s_sb[part][:], in_=states[part])
-        for i in range(1, B_BUFS):
+        for i in range(2, 2 * G1, 2):
             load_b(i)
 
         u_words = u_sb[:].bitcast(F32)
@@ -259,8 +263,6 @@ def tile_linearrecurrentunitcell_w_kernel(
                     start=(g == 0),
                     stop=(g == G1 - 1),
                 )
-            if i + B_BUFS < 2 * G1:
-                load_b(i + B_BUFS)
 
         scaled = {}
 
@@ -356,8 +358,8 @@ def tile_linearrecurrentunitcell_w_kernel(
             else:
                 spread_gamma(2 * (g - NB1))
                 spread_gamma(2 * (g - NB1) + 1)
-        for j in range(C_BUFS):
-            load_c(j)
+        for j in range(0, 2 * G2 - 2, 2):
+            load_c(j, 2)
 
         for n in range(NB1):
             scale_by_gamma(0, n)
@@ -372,25 +374,11 @@ def tile_linearrecurrentunitcell_w_kernel(
             scale_by_gamma(1, n)
         open_y()
         last = 2 * G2 - 1
-        pieces = []
-
-        def load_pieces():
-            for k in range(N_IN // PIECE):
-                piece = cp.tile([P, PIECE], U32, name="piece", tag="piece", align_bytes=256)
-                nc.sync.dma_start(
-                    out=piece[:].bitcast(I32),
-                    in_=c_words[1][G2 - 1]
-                    .rearrange("p n t -> p (n t)")[:, 4 * PIECE * k : 4 * PIECE * (k + 1)]
-                    .bitcast(I32),
-                )
-                pieces.append(piece)
-
+        load_c(last - 1, 1)
+        load_c(last, 1)
         for j in range(last):
             stage2(j)
-            if j + C_BUFS < last:
-                load_c(j + C_BUFS)
-            if j + C_BUFS == last:
-                load_pieces()
+            if j == 2:
                 for part in range(2):
                     nc.sync.dma_start(out=x_out[part], in_=x_sb[part][:])
             if j < 2:
@@ -405,5 +393,5 @@ def tile_linearrecurrentunitcell_w_kernel(
         for k in range(N_IN // PIECE):
             for r in range(per_piece):
                 n = per_piece * k + r
-                stage2_pass(last, n, pieces[k][:, BANK * r : BANK * (r + 1)])
+                stage2_pass(last, n, c_tiles[last][:, BANK * n : BANK * (n + 1)])
             finish_y(k)

@@ -80,8 +80,11 @@ def tile_linearrecurrentunitcell_w_kernel(
         pc = const.tile([P, 2, N_IN], U8, name="pc", align_bytes=256)
         for small in (nu_t, th_t, gd_t):
             nc.vector.memset(small[:].bitcast(I32), 0)
-        nc.vector.memset(pb[:].rearrange("p s n -> p (s n)").bitcast(I32), 0)
-        nc.vector.memset(pc[:].rearrange("p s n -> p (s n)").bitcast(I32), 0)
+        nc.vector.memset(pb[:, 0, :].bitcast(I32), 0)
+        nc.vector.memset(pc[:, 0, :].bitcast(I32), 0)
+        nc.vector.memset(pb[:, 2, :].bitcast(I32), 0)
+        nc.vector.memset(pb[:, 1, :].bitcast(I32), 0)
+        nc.vector.memset(pc[:, 1, :].bitcast(I32), 0)
 
         u_sb = const.tile([P, N_IN], BF16, name="u_sb", align_bytes=256)
         u_grp = const.tile([P, N_IN], BF16, name="u_grp", align_bytes=64)
@@ -104,20 +107,20 @@ def tile_linearrecurrentunitcell_w_kernel(
         nc.scalar.dma_start(out=gd_t[0:4, :], in_=gamma.rearrange("(r c) -> r c", c=BANK))
         nc.scalar.dma_start(out=gd_t[4:10, :], in_=D.rearrange("(r c) -> r c", c=BANK))
 
-        def load_planes(planes, slot, first, count, src, g0):
+        def load_planes(dma, view, planes, slot, first, count, src, g0):
             for q in (0, 2, 1, 3):
-                nc.sync.dma_start(
-                    out=planes[32 * q + first : 32 * q + first + 4 * count, slot, :].bitcast(I32),
-                    in_=src[g0 : g0 + count, 4 * q : 4 * q + 4, :].bitcast(I32),
+                dma(
+                    out=planes[32 * q + first : 32 * q + first + 4 * count, slot, :].bitcast(view),
+                    in_=src[g0 : g0 + count, 4 * q : 4 * q + 4, :].bitcast(view),
                 )
 
-        load_planes(pb, 0, 0, 4, B_re_scales, 0)
+        load_planes(nc.gpsimd.dma_start, F32, pc, 0, 0, 4, C_re_scales, 0)
         make_identity(nc, ident_b[:])
-        load_planes(pb, 2, 0, 2, B_re_scales, 4)
-        load_planes(pb, 1, 0, 4, B_im_scales, 0)
-        load_planes(pb, 2, 8, 2, B_im_scales, 4)
-        load_planes(pc, 0, 0, 4, C_re_scales, 0)
-        load_planes(pc, 1, 0, 4, C_im_scales, 0)
+        load_planes(nc.sync.dma_start, I32, pb, 0, 0, 4, B_re_scales, 0)
+        load_planes(nc.sync.dma_start, I32, pb, 2, 0, 2, B_re_scales, 4)
+        load_planes(nc.sync.dma_start, I32, pb, 1, 0, 4, B_im_scales, 0)
+        load_planes(nc.sync.dma_start, I32, pb, 2, 8, 2, B_im_scales, 4)
+        load_planes(nc.sync.dma_start, I32, pc, 1, 0, 4, C_im_scales, 0)
 
         b_tiles = {}
         c_tiles = {}

from contextlib import ExitStack

import concourse.mybir as mybir
from concourse.masks import make_identity

F32 = mybir.dt.float32
BF16 = mybir.dt.bfloat16
U32 = mybir.dt.uint32
U8 = mybir.dt.uint8
I32 = mybir.dt.int32
FP8X4 = mybir.dt.float8_e4m3fn_x4
ALU = mybir.AluOpType
ACT = mybir.ActivationFunctionType

P = 128
N_IN = 3072
H = 2048
BANK = 512
G1 = N_IN // 512
G2 = H // 512
NB1 = H // BANK
NB2 = N_IN // BANK
PIECE = 1024
B_BYTES = 4 * H
C_BYTES = 4 * N_IN
RING = 15 * B_BYTES

FLOPS = 2 * P * 4 * N_IN * H


def tile_linearrecurrentunitcell_w_kernel(
    tc,
    inputs,
    state_re,
    state_im,
    B_re_words,
    B_re_scales,
    B_im_words,
    B_im_scales,
    C_re_words,
    C_re_scales,
    C_im_words,
    C_im_scales,
    D,
    nu,
    theta,
    gamma,
    out_0,
    out_1,
    out_2,
):
    nc = tc.nc
    b_words = (B_re_words, B_im_words)
    c_words = (C_re_words, C_im_words)
    states = (state_re, state_im)
    x_out = (out_1, out_2)

    with ExitStack() as ctx:
        const = ctx.enter_context(tc.tile_pool(name="const", bufs=1))
        work = ctx.enter_context(tc.tile_pool(name="work", bufs=3))
        ring = ctx.enter_context(tc.tile_pool(name="ring", bufs=1))
        ps = ctx.enter_context(tc.psum_pool(name="ps", bufs=1))
        ctx.enter_context(tc.manual_schedule())

        scratch_count = [0]

        def scratch(shape, dtype, name):
            bank = 4 + scratch_count[0] % 4
            scratch_count[0] += 1
            return ps.tile(shape, dtype, name=name, tag="b%d" % bank)

        ident_f = const.tile([P, P], F32, name="ident_f")
        make_identity(nc, ident_f[:])
        ident_b = const.tile([P, P], BF16, name="ident_b")

        nu_t = const.tile([P, P], BF16, name="nu_t")
        th_t = const.tile([P, P], BF16, name="th_t")
        gd_t = const.tile([P, BANK], BF16, name="gd_t")
        pb = const.tile([P, 3, H], U8, name="pb", align_bytes=256)
        pc = const.tile([P, 2, N_IN], U8, name="pc", align_bytes=256)
        for small in (nu_t, th_t, gd_t):
            nc.vector.memset(small[:].bitcast(I32), 0)
        nc.vector.memset(pb[:, 0, :].bitcast(I32), 0)
        nc.vector.memset(pc[:, 0, :].bitcast(I32), 0)
        nc.vector.memset(pb[:, 2, :].bitcast(I32), 0)
        nc.vector.memset(pb[:, 1, :].bitcast(I32), 0)
        nc.vector.memset(pc[:, 1, :].bitcast(I32), 0)

        u_sb = const.tile([P, N_IN], BF16, name="u_sb", align_bytes=256)
        u_grp = const.tile([P, N_IN], BF16, name="u_grp", align_bytes=64)
        uq_w = const.tile([P, G1 * P], U32, name="uq_w", align_bytes=64)
        uq_s = const.tile([P, G1 * P], U8, name="uq_s", align_bytes=64)
        s_sb = [const.tile([P, H], BF16, name="s_sb%d" % part, align_bytes=256) for part in range(2)]
        x_sb = [const.tile([P, H], F32, name="x_sb%d" % part, align_bytes=256) for part in range(2)]
        xq_w = [const.tile([P, G2 * P], U32, name="xq_w%d" % part, align_bytes=64) for part in range(2)]
        xq_s = [const.tile([P, G2 * P], U8, name="xq_s%d" % part, align_bytes=64) for part in range(2)]
        mag = const.tile([P, P], F32, name="mag")
        lam_re = const.tile([P, P], F32, name="lam_re")
        lam_im = const.tile([P, P], F32, name="lam_im")
        lam_col = const.tile([P, 2, H // P], F32, name="lam_col")
        gam_b = const.tile([P, H], BF16, name="gam_b")
        du = const.tile([P, N_IN], F32, name="du")

        nc.sync.dma_start(out=u_sb[:], in_=inputs)
        nc.scalar.dma_start(out=nu_t[0 : H // P, :], in_=nu.rearrange("(r c) -> r c", c=P))
        nc.scalar.dma_start(out=th_t[0 : H // P, :], in_=theta.rearrange("(r c) -> r c", c=P))
        nc.scalar.dma_start(out=gd_t[0:4, :], in_=gamma.rearrange("(r c) -> r c", c=BANK))
        nc.scalar.dma_start(out=gd_t[4:10, :], in_=D.rearrange("(r c) -> r c", c=BANK))

        def load_planes(dma, view, planes, slot, first, count, src, g0):
            for q in (0, 2, 1, 3):
                dma(
                    out=planes[32 * q + first : 32 * q + first + 4 * count, slot, :].bitcast(view),
                    in_=src[g0 : g0 + count, 4 * q : 4 * q + 4, :].bitcast(view),
                )

        load_planes(nc.gpsimd.dma_start, F32, pc, 0, 0, 4, C_re_scales, 0)
        make_identity(nc, ident_b[:])
        load_planes(nc.sync.dma_start, I32, pb, 0, 0, 4, B_re_scales, 0)
        load_planes(nc.sync.dma_start, I32, pb, 2, 0, 2, B_re_scales, 4)
        load_planes(nc.sync.dma_start, I32, pb, 1, 0, 4, B_im_scales, 0)
        load_planes(nc.sync.dma_start, I32, pb, 2, 8, 2, B_im_scales, 4)
        load_planes(nc.sync.dma_start, I32, pc, 1, 0, 4, C_im_scales, 0)

        b_tiles = {}
        c_tiles = {}

        def load_b(i):
            part, g = divmod(i, G1)
            bw = ring.tile([P, 2, H], U32, name="bw%d" % i, tag="bw%d" % i, align_bytes=256, offset=B_BYTES * i)
            nc.sync.dma_start(
                out=bw[:].bitcast(I32),
                in_=b_words[part][g : g + 2].rearrange("g p n t -> p g (n t)").bitcast(I32),
            )
            for r in range(2):
                b_tiles[i + r] = bw[:, r, :]

        def load_c(j, count):
            part, g = divmod(j, G2)
            cw = ring.tile(
                [P, count, N_IN], U32, name="cw%d" % j, tag="cw%d" % j, align_bytes=256,
                offset=(2 * G1 * B_BYTES + j * C_BYTES) % RING,
            )
            nc.sync.dma_start(
                out=cw[:].bitcast(I32),
                in_=c_words[part][g : g + count].rearrange("g p n t -> p g (n t)").bitcast(I32),
            )
            for r in range(count):
                c_tiles[j + r] = cw[:, r, :]

        load_b(0)
        for part in range(2):
            nc.sync.dma_start(out=s_sb[part][:], in_=states[part])
        for i in range(2, 2 * G1, 2):
            load_b(i)

        u_words = u_sb[:].bitcast(F32)
        u_grp_words = u_grp[:].bitcast(F32)

        def u_transposes(j):
            ut = scratch([P, 2, 2, P], F32, "ut")
            for gg in range(2):
                g = 2 * j + gg
                for half in range(2):
                    nc.tensor.transpose(
                        ut[:, gg, half, :],
                        u_words[:, 256 * g + half : 256 * (g + 1) : 2],
                        ident_f[:],
                    )
            nc.vector.tensor_copy(
                out=u_grp_words[:, 512 * j : 512 * (j + 1)].rearrange(
                    "p (g m h) -> p g m h", g=2, h=2
                ),
                in_=ut[:].rearrange("p g h m -> p g m h"),
            )

        def u_quantise(j):
            nc.vector.quantize_mx(
                out=uq_w[:, 256 * j : 256 * (j + 1)].bitcast(FP8X4),
                scales=uq_s[:, 256 * j : 256 * (j + 1)],
                in_=u_grp[:, 1024 * j : 1024 * (j + 1)],
            )

        u_transposes(0)
        u_transposes(1)
        u_quantise(0)
        u_transposes(2)
        u_quantise(1)
        u_quantise(2)

        nc.scalar.activation(out=mag[:], in_=nu_t[:], func=ACT.Exp)
        nc.scalar.activation(out=mag[:], in_=mag[:], func=ACT.Exp, scale=-1.0)
        nc.scalar.activation(out=lam_im[:], in_=th_t[:], func=ACT.Sin)
        nc.scalar.activation(out=lam_re[:], in_=th_t[:], func=ACT.Sin, scale=0.5)
        nc.scalar.activation(out=lam_re[:], in_=lam_re[:], func=ACT.Square)
        nc.vector.tensor_tensor(out=lam_im[:], in0=lam_im[:], in1=mag[:], op=ALU.mult)
        nc.vector.tensor_scalar(
            out=lam_re[:], in0=lam_re[:], scalar1=-2.0, scalar2=1.0, op0=ALU.mult, op1=ALU.add
        )
        nc.vector.tensor_tensor(out=lam_re[:], in0=lam_re[:], in1=mag[:], op=ALU.mult)

        lam_ps = scratch([P, 2, P], F32, "lam_ps")
        nc.tensor.transpose(lam_ps[:, 0, :], lam_re[:], ident_f[:])
        nc.tensor.transpose(lam_ps[:, 1, :], lam_im[:], ident_f[:])
        nc.vector.tensor_copy(out=lam_col[:], in_=lam_ps[:, :, 0 : H // P])

        lam_banks = {}

        def spread_lambda(c):
            banks = []
            for part in range(2):
                bank = scratch([P, BANK], F32, "lam_bank")
                for r in range(4):
                    nc.tensor.transpose(
                        bank[:, P * r : P * (r + 1)],
                        lam_col[:, part, 4 * c + r : 4 * c + r + 1].to_broadcast([P, P]),
                        ident_f[:],
                    )
                banks.append(bank)
            lam_banks[c] = banks

        def rotate_state(c):
            cols = slice(BANK * c, BANK * (c + 1))
            l_re, l_im = lam_banks[c]
            t_re = work.tile([P, BANK], F32, name="t_re", tag="t_rot", bufs=3)
            t_im = work.tile([P, BANK], F32, name="t_im", tag="t_rot", bufs=3)
            nc.vector.tensor_tensor(out=x_sb[0][:, cols], in0=l_re[:], in1=s_sb[0][:, cols], op=ALU.mult)
            nc.vector.tensor_tensor(out=t_im[:], in0=l_re[:], in1=s_sb[1][:, cols], op=ALU.mult)
            nc.vector.tensor_tensor(out=t_re[:], in0=l_im[:], in1=s_sb[1][:, cols], op=ALU.mult)
            nc.vector.tensor_tensor(out=x_sb[1][:, cols], in0=l_im[:], in1=s_sb[0][:, cols], op=ALU.mult)
            nc.vector.tensor_tensor(out=x_sb[0][:, cols], in0=x_sb[0][:, cols], in1=t_re[:], op=ALU.subtract)
            nc.vector.tensor_tensor(out=x_sb[1][:, cols], in0=x_sb[1][:, cols], in1=t_im[:], op=ALU.add)

        def spread_gamma(c):
            g_ps = scratch([P, BANK], F32, "g_ps")
            nc.tensor.matmul(
                out=g_ps[:],
                lhsT=ident_b[:, c : c + 1].to_broadcast([P, P]),
                rhs=gd_t[:],
                start=True,
                stop=True,
            )
            nc.scalar.copy(out=gam_b[:, BANK * c : BANK * (c + 1)], in_=g_ps[:])

        acc = {}

        def b_plane(part, g):
            if g < 4:
                return part, 4 * g
            return 2, 8 * part + 4 * (g - 4)

        def stage1(i):
            part, g = divmod(i, G1)
            if g == 0:
                for n in range(NB1):
                    acc[(part, n)] = ps.tile([P, BANK], F32, name="acc", tag="b%d" % n)
            slot, k = b_plane(part, g)
            for n in range(NB1):
                cols = slice(BANK * n, BANK * (n + 1))
                nc.tensor.matmul_mx(
                    out=acc[(part, n)][:],
                    lhsT=uq_w[:, P * g : P * (g + 1)].bitcast(FP8X4),
                    lhsT_scale=uq_s[:, P * g : P * (g + 1)],
                    rhs=b_tiles[i][:, cols].bitcast(FP8X4),
                    rhs_scale=pb[k:P, slot, cols],
                    start=(g == 0),
                    stop=(g == G1 - 1),
                )

        scaled = {}

        def scale_by_gamma(part, n):
            cols = slice(BANK * n, BANK * (n + 1))
            sc = work.tile([P, BANK], F32, name="sc", tag="sc", bufs=4)
            nc.vector.tensor_tensor(out=sc[:], in0=acc[(part, n)][:], in1=gam_b[:, cols], op=ALU.mult)
            scaled[(part, n)] = sc

        x_t = {}

        def finish_x(part, n):
            cols = slice(BANK * n, BANK * (n + 1))
            nc.vector.tensor_tensor(
                out=x_sb[part][:, cols], in0=scaled[(part, n)][:], in1=x_sb[part][:, cols], op=ALU.add
            )
            x_bf = work.tile([P, BANK], BF16, name="x_bf", tag="x_bf", bufs=3)
            nc.scalar.activation(
                out=x_bf[:], in_=x_sb[part][:, cols], func=ACT.Copy, scale=(1.0 if part == 0 else -1.0)
            )
            if part == 0:
                xt = scratch([P, 4, P], BF16, "xt")
            else:
                xt = ps.tile([P, 4, P], BF16, name="xt", tag="b%d" % (6 + n % 2))
            for t in range(4):
                nc.tensor.transpose(xt[:, t, :], x_bf[:, t:BANK:4], ident_b[:])
            x_t[(part, n)] = xt

        def quantise_x(part, n):
            x_grp = work.tile([P, BANK], BF16, name="x_grp", tag="x_grp", bufs=3, align_bytes=64)
            nc.scalar.copy(
                out=x_grp[:].rearrange("p (m t) -> p m t", t=4),
                in_=x_t[(part, n)][:].rearrange("p t m -> p m t"),
            )
            nc.vector.quantize_mx(
                out=xq_w[part][:, P * n : P * (n + 1)].bitcast(FP8X4),
                scales=xq_s[part][:, P * n : P * (n + 1)],
                in_=x_grp[:],
            )

        y_acc = {}

        def open_y():
            for n in range(NB2):
                y_acc[n] = ps.tile([P, BANK], F32, name="y_acc", tag="b%d" % n)

        def stage2_pass(j, n, words):
            part, g = divmod(j, G2)
            nc.tensor.matmul_mx(
                out=y_acc[n][:],
                lhsT=xq_w[part][:, P * g : P * (g + 1)].bitcast(FP8X4),
                lhsT_scale=xq_s[part][:, P * g : P * (g + 1)],
                rhs=words.bitcast(FP8X4),
                rhs_scale=pc[4 * g : P, part, BANK * n : BANK * (n + 1)],
                start=(j == 0),
                stop=(j == 2 * G2 - 1),
            )

        def stage2(j):
            for n in range(NB2):
                stage2_pass(j, n, c_tiles[j][:, BANK * n : BANK * (n + 1)])

        def skip_term(c):
            cols = slice(BANK * c, BANK * (c + 1))
            d_ps = ps.tile([P, BANK], F32, name="d_ps", tag="b%d" % (6 + c % 2))
            nc.tensor.matmul(
                out=d_ps[:],
                lhsT=ident_b[:, 4 + c : 5 + c].to_broadcast([P, P]),
                rhs=gd_t[:],
                start=True,
                stop=True,
            )
            nc.vector.tensor_tensor(out=du[:, cols], in0=d_ps[:], in1=u_sb[:, cols], op=ALU.mult)

        def finish_y(k):
            y_sb = work.tile([P, PIECE], F32, name="y_sb", tag="y_sb", bufs=3, align_bytes=256)
            for r in range(PIECE // BANK):
                n = (PIECE // BANK) * k + r
                nc.vector.tensor_tensor(
                    out=y_sb[:, BANK * r : BANK * (r + 1)],
                    in0=y_acc[n][:],
                    in1=du[:, BANK * n : BANK * (n + 1)],
                    op=ALU.add,
                )
            nc.sync.dma_start(out=out_0[:, PIECE * k : PIECE * (k + 1)], in_=y_sb[:])

        for g in range(G1):
            if g < NB1:
                spread_lambda(g)
            stage1(g)
            if g < NB1:
                rotate_state(g)
            else:
                spread_gamma(2 * (g - NB1))
                spread_gamma(2 * (g - NB1) + 1)
        for j in range(0, 2 * G2 - 2, 2):
            load_c(j, 2)

        for n in range(NB1):
            scale_by_gamma(0, n)
        for g in range(G1):
            stage1(G1 + g)
            if g < NB1:
                finish_x(0, g)
            if 1 <= g <= NB1:
                quantise_x(0, g - 1)

        for n in range(NB1):
            scale_by_gamma(1, n)
        open_y()
        last = 2 * G2 - 1
        load_c(last - 1, 1)
        load_c(last, 1)
        for j in range(last):
            stage2(j)
            if j == 2:
                for part in range(2):
                    nc.sync.dma_start(out=x_out[part], in_=x_sb[part][:])
            if j < 2:
                finish_x(1, 2 * j)
                finish_x(1, 2 * j + 1)
                quantise_x(1, 2 * j)
                quantise_x(1, 2 * j + 1)
            elif j < 5:
                skip_term(2 * (j - 2))
                skip_term(2 * (j - 2) + 1)
        per_piece = PIECE // BANK
        for k in range(N_IN // PIECE):
            for r in range(per_piece):
                n = per_piece * k + r
                stage2_pass(last, n, c_tiles[last][:, BANK * n : BANK * (n + 1)])
            finish_y(k)
